import numpy as np
import ml_dtypes

BF16 = ml_dtypes.bfloat16


def bf(x):
    return np.asarray(x, np.float32).astype(BF16)


def f32(x):
    return np.asarray(x, np.float32)


def f64(x):
    return np.asarray(x).astype(np.float64)


def striped(idx):
    return np.tile(idx.reshape(-1, 16).T, (8, 1))


D, S, N, HALF = 128, 512, 512, 128


def setup_inputs():
    return {
        "x": bf(np.random.standard_normal((D, S))),
        "wq": bf(np.sqrt(2.0 / D) * np.random.standard_normal((D, D))),
        "bq": f32(0.1 * np.random.standard_normal((D, 1))),
        "wk": bf(np.sqrt(2.0 / D) * np.random.standard_normal((D, D))),
        "wv": bf(np.random.standard_normal((D, D)) / np.sqrt(D)),
        "bv": f32(0.1 * np.random.standard_normal((D, 1))),
        "offs": striped(np.random.permutation(S)[:N]),
    }


def reference(x, wq, bq, wk, wv, bv, offs):
    idx = offs[:16].T.reshape(-1)
    xo = f64(x)[:, idx]
    q = f64(wq).T @ xo + f64(bq)
    k = f64(wk).T @ xo
    v = f64(wv).T @ xo + f64(bv)
    s = (q.T @ k) / np.sqrt(D)
    pos = np.arange(N)
    near = ((pos[None, :] - pos[:, None] + HALF) % N) <= 2 * HALF
    e = np.where(near, np.exp(s - s.max(axis=1, keepdims=True)), 0.0)
    p = e / e.sum(axis=1, keepdims=True)
    return v @ p.T

@@ -1,0 +1,136 @@
+import math
+
+import concourse.mybir as mybir
+
+BF16, F32, I32, U16 = mybir.dt.bfloat16, mybir.dt.float32, mybir.dt.int32, mybir.dt.uint16
+FUNC = mybir.ActivationFunctionType
+ALU = mybir.AluOpType
+
+D = 128
+N = 512
+HALF = 128
+BLOCK = 128
+N_BLOCKS = N // BLOCK
+BAND = BLOCK + 2 * HALF
+BAND_BLOCKS = BAND // BLOCK
+MASKED = -1.0e30
+
+FLOPS = 3 * 2 * D * D * N + 2 * 2 * D * N * (2 * HALF + 1)
+
+
+def unwrapped_runs(first, width, ring):
+    first = first % ring
+    head = min(width, ring - first)
+    runs = [(0, first, head)]
+    if head < width:
+        runs.append((head, 0, width - head))
+    return runs
+
+
+def tile_slidingwindowattention_kernel(tc, x, wq, bq, wk, wv, bv, offs, out):
+    nc = tc.nc
+    with (
+        tc.tile_pool(name="held", bufs=1) as held,
+        tc.tile_pool(name="per_block", bufs=N_BLOCKS) as per_block,
+        tc.psum_pool(name="score_banks", bufs=N_BLOCKS) as score_banks,
+        tc.psum_pool(name="other_banks", bufs=8 - N_BLOCKS) as other_banks,
+    ):
+        offsets = held.tile([D, N // 16], U16, name="offsets")
+        nc.sync.dma_start(offsets[:], offs)
+        x_sb = held.tile([D, N], BF16, name="x_sb")
+        nc.sync.dma_start(x_sb[:], x)
+        wq_sb = held.tile([D, D], BF16, name="wq_sb")
+        nc.scalar.dma_start(wq_sb[:], wq)
+        wk_sb = held.tile([D, D], BF16, name="wk_sb")
+        nc.scalar.dma_start(wk_sb[:], wk)
+        wv_sb = held.tile([D, D], BF16, name="wv_sb")
+        nc.scalar.dma_start(wv_sb[:], wv)
+        bq_sb = held.tile([D, 1], F32, name="bq_sb")
+        nc.sync.dma_start(bq_sb[:], bq)
+        bv_sb = held.tile([D, 1], F32, name="bv_sb")
+        nc.sync.dma_start(bv_sb[:], bv)
+
+        scratch = held.tile([D, 1], F32, name="scratch")
+        nc.vector.memset(scratch[:], 0.0)
+        nc.scalar.activation(scratch[:], scratch[:], FUNC.Exp)
+
+        ahead = held.tile([BLOCK, BLOCK], I32, name="ahead")
+        nc.gpsimd.iota(ahead[:], pattern=[[1, BLOCK]], base=0, channel_multiplier=-1)
+        identity = held.tile([BLOCK, BLOCK], BF16, name="identity")
+        nc.vector.tensor_scalar(identity[:], ahead[:], 0.0, None, op0=ALU.is_equal)
+
+        band_mask = held.tile([BLOCK, BAND], BF16, name="band_mask")
+        nc.vector.tensor_scalar(band_mask[:, 0:BLOCK], ahead[:], 0.0, MASKED, op0=ALU.is_lt, op1=ALU.mult)
+        nc.vector.memset(band_mask[:, BLOCK : BAND - BLOCK], 0.0)
+        nc.vector.tensor_scalar(band_mask[:, BAND - BLOCK : BAND], ahead[:], 0.0, MASKED, op0=ALU.is_gt, op1=ALU.mult)
+
+        scores = []
+        for b in range(N_BLOCKS):
+            s_ps = score_banks.tile([BLOCK, BAND], F32, name="s_ps")
+            nc.tensor.matmul(s_ps[:], identity[:], band_mask[:], start=True, stop=False)
+            scores.append(s_ps)
+
+        q_ps = other_banks.tile([D, N], F32, name="q_ps", tag="bank")
+        nc.tensor.matmul(q_ps[:], wq_sb[:], x_sb[:].indirect(offsets[:]), start=True, stop=True)
+        k_ps = other_banks.tile([D, N], F32, name="k_ps", tag="bank")
+        nc.tensor.matmul(k_ps[:], wk_sb[:], x_sb[:].indirect(offsets[:]), start=True, stop=True)
+        v_ps = other_banks.tile([D, N], F32, name="v_ps", tag="bank")
+        nc.tensor.matmul(v_ps[:], wv_sb[:], x_sb[:].indirect(offsets[:]), start=True, stop=True)
+
+        q_sb = held.tile([D, N], BF16, name="q_sb")
+        nc.vector.tensor_scalar(q_sb[:], q_ps[:], bq_sb[:, 0:1], 1.0 / math.sqrt(D), op0=ALU.add, op1=ALU.mult)
+        k_sb = held.tile([D, N], BF16, name="k_sb")
+        nc.scalar.copy(k_sb[:], k_ps[:])
+        v_sb = held.tile([D, N], BF16, name="v_sb")
+        nc.scalar.activation(v_sb[:], v_ps[:], FUNC.Identity, bias=bv_sb[:, 0:1])
+
+        for b in range(N_BLOCKS):
+            runs = unwrapped_runs(b * BLOCK - HALF, BAND, N)
+            for at, first, width in runs:
+                nc.tensor.matmul(
+                    scores[b][:, at : at + width],
+                    q_sb[:, b * BLOCK : (b + 1) * BLOCK],
+                    k_sb[:, first : first + width],
+                    start=False,
+                    stop=(at + width == BAND),
+                )
+
+        vT_ps = other_banks.tile([BLOCK, N], BF16, name="vT_ps", tag="bank")
+        for c in range(N_BLOCKS):
+            cols = slice(c * BLOCK, (c + 1) * BLOCK)
+            nc.tensor.transpose(vT_ps[:, cols], v_sb[:, cols], identity[:])
+        vT_sb = held.tile([BLOCK, N], BF16, name="vT_sb")
+        nc.vector.tensor_copy(vT_sb[:], vT_ps[:])
+
+        for b in range(N_BLOCKS):
+            s_ps = scores[b]
+            neg_max = per_block.tile([BLOCK, 1], F32, name="neg_max")
+            nc.vector.reduce_max(neg_max[:], s_ps[:], axis=mybir.AxisListType.X, negate=True)
+            e_sb = per_block.tile([BLOCK, BAND], F32, name="e_sb")
+            e_sum = per_block.tile([BLOCK, 1], F32, name="e_sum")
+            nc.scalar.activation(e_sb[:], s_ps[:], FUNC.Exp, bias=neg_max[:, 0:1], accum_out=e_sum[:, 0:1])
+            inv_sum = per_block.tile([BLOCK, 1], F32, name="inv_sum")
+            nc.vector.reciprocal(inv_sum[:], e_sum[:])
+            p_sb = per_block.tile([BLOCK, BAND], BF16, name="p_sb")
+            nc.vector.tensor_scalar(p_sb[:], e_sb[:], inv_sum[:, 0:1], None, op0=ALU.mult)
+
+            pT_ps = other_banks.tile([BLOCK, BAND], BF16, name="pT_ps", tag="bank")
+            for i in range(BAND_BLOCKS):
+                cols = slice(i * BLOCK, (i + 1) * BLOCK)
+                nc.tensor.transpose(pT_ps[:, cols], p_sb[:, cols], identity[:])
+            pT_sb = per_block.tile([BLOCK, BAND], BF16, name="pT_sb")
+            nc.scalar.copy(pT_sb[:], pT_ps[:])
+
+            o_ps = other_banks.tile([D, BLOCK], F32, name="o_ps", tag="bank")
+            for i in range(BAND_BLOCKS):
+                c = (b - HALF // BLOCK + i) % N_BLOCKS
+                nc.tensor.matmul(
+                    o_ps[:],
+                    vT_sb[:, c * BLOCK : (c + 1) * BLOCK],
+                    pT_sb[:, i * BLOCK : (i + 1) * BLOCK],
+                    start=(i == 0),
+                    stop=(i == BAND_BLOCKS - 1),
+                )
+            o_sb = per_block.tile([D, BLOCK], F32, name="o_sb")
+            nc.vector.tensor_copy(o_sb[:], o_ps[:])
+            nc.sync.dma_start(out[:, b * BLOCK : (b + 1) * BLOCK], o_sb[:])

@@ -13,6 +13,7 @@ BLOCK = 128
 N_BLOCKS = N // BLOCK
 BAND = BLOCK + 2 * HALF
 BAND_BLOCKS = BAND // BLOCK
+N_WARM = 14
 MASKED = -1.0e30
 
 FLOPS = 3 * 2 * D * D * N + 2 * 2 * D * N * (2 * HALF + 1)
@@ -35,20 +36,26 @@ def tile_slidingwindowattention_kernel(tc, x, wq, bq, wk, wv, bv, offs, out):
         tc.psum_pool(name="score_banks", bufs=N_BLOCKS) as score_banks,
         tc.psum_pool(name="other_banks", bufs=8 - N_BLOCKS) as other_banks,
     ):
-        offsets = held.tile([D, N // 16], U16, name="offsets")
-        nc.sync.dma_start(offsets[:], offs)
         x_sb = held.tile([D, N], BF16, name="x_sb")
         nc.sync.dma_start(x_sb[:], x)
+        offsets = held.tile([D, N // 16], U16, name="offsets")
+        nc.sync.dma_start(offsets[:], offs)
         wq_sb = held.tile([D, D], BF16, name="wq_sb")
         nc.scalar.dma_start(wq_sb[:], wq)
+        bq_sb = held.tile([D, 1], F32, name="bq_sb")
+        nc.scalar.dma_start(bq_sb[:], bq)
         wk_sb = held.tile([D, D], BF16, name="wk_sb")
-        nc.scalar.dma_start(wk_sb[:], wk)
+        nc.sync.dma_start(wk_sb[:], wk)
         wv_sb = held.tile([D, D], BF16, name="wv_sb")
         nc.scalar.dma_start(wv_sb[:], wv)
-        bq_sb = held.tile([D, 1], F32, name="bq_sb")
-        nc.sync.dma_start(bq_sb[:], bq)
         bv_sb = held.tile([D, 1], F32, name="bv_sb")
         nc.sync.dma_start(bv_sb[:], bv)
+
+        zeros = held.tile([D, BLOCK], BF16, name="zeros")
+        nc.vector.memset(zeros[:], 0.0)
+        warm_ps = other_banks.tile([D, BLOCK], F32, name="warm_ps", tag="bank")
+        for w in range(N_WARM):
+            nc.tensor.matmul(warm_ps[:], zeros[:], zeros[:], start=True, stop=True)
 
         scratch = held.tile([D, 1], F32, name="scratch")
         nc.vector.memset(scratch[:], 0.0)
@@ -64,12 +71,6 @@ def tile_slidingwindowattention_kernel(tc, x, wq, bq, wk, wv, bv, offs, out):
         nc.vector.memset(band_mask[:, BLOCK : BAND - BLOCK], 0.0)
         nc.vector.tensor_scalar(band_mask[:, BAND - BLOCK : BAND], ahead[:], 0.0, MASKED, op0=ALU.is_gt, op1=ALU.mult)
 
-        scores = []
-        for b in range(N_BLOCKS):
-            s_ps = score_banks.tile([BLOCK, BAND], F32, name="s_ps")
-            nc.tensor.matmul(s_ps[:], identity[:], band_mask[:], start=True, stop=False)
-            scores.append(s_ps)
-
         q_ps = other_banks.tile([D, N], F32, name="q_ps", tag="bank")
         nc.tensor.matmul(q_ps[:], wq_sb[:], x_sb[:].indirect(offsets[:]), start=True, stop=True)
         k_ps = other_banks.tile([D, N], F32, name="k_ps", tag="bank")
@@ -82,52 +83,56 @@ def tile_slidingwindowattention_kernel(tc, x, wq, bq, wk, wv, bv, offs, out):
         k_sb = held.tile([D, N], BF16, name="k_sb")
         nc.scalar.copy(k_sb[:], k_ps[:])
         v_sb = held.tile([D, N], BF16, name="v_sb")
-        nc.scalar.activation(v_sb[:], v_ps[:], FUNC.Identity, bias=bv_sb[:, 0:1])
+        nc.vector.tensor_scalar(v_sb[:], v_ps[:], bv_sb[:, 0:1], None, op0=ALU.add)
 
+
+        s_ps = [score_banks.tile([BLOCK, BAND], F32, name="s_ps") for b in range(N_BLOCKS)]
         for b in range(N_BLOCKS):
-            runs = unwrapped_runs(b * BLOCK - HALF, BAND, N)
-            for at, first, width in runs:
+            for at, first, width in unwrapped_runs(b * BLOCK - HALF, BAND, N):
                 nc.tensor.matmul(
-                    scores[b][:, at : at + width],
+                    s_ps[b][:, at : at + width],
                     q_sb[:, b * BLOCK : (b + 1) * BLOCK],
                     k_sb[:, first : first + width],
-                    start=False,
-                    stop=(at + width == BAND),
+                    start=(at == 0),
+                    stop=False,
                 )
+            nc.tensor.matmul(s_ps[b][:], identity[:], band_mask[:], start=False, stop=True)
 
         vT_ps = other_banks.tile([BLOCK, N], BF16, name="vT_ps", tag="bank")
         for c in range(N_BLOCKS):
             cols = slice(c * BLOCK, (c + 1) * BLOCK)
             nc.tensor.transpose(vT_ps[:, cols], v_sb[:, cols], identity[:])
+
+        e_sb = [per_block.tile([BLOCK, BAND], F32, name="e_sb") for b in range(N_BLOCKS)]
+        e_sum = [per_block.tile([BLOCK, 1], F32, name="e_sum") for b in range(N_BLOCKS)]
+        for b in range(N_BLOCKS):
+            neg_max = per_block.tile([BLOCK, 1], F32, name="neg_max")
+            nc.vector.reduce_max(neg_max[:], s_ps[b][:], axis=mybir.AxisListType.X, negate=True)
+            nc.scalar.activation(e_sb[b][:], s_ps[b][:], FUNC.Exp, bias=neg_max[:, 0:1], accum_out=e_sum[b][:, 0:1])
+
         vT_sb = held.tile([BLOCK, N], BF16, name="vT_sb")
         nc.vector.tensor_copy(vT_sb[:], vT_ps[:])
 
+        pT_sb = [per_block.tile([BLOCK, BAND], BF16, name="pT_sb") for b in range(N_BLOCKS)]
         for b in range(N_BLOCKS):
-            s_ps = scores[b]
-            neg_max = per_block.tile([BLOCK, 1], F32, name="neg_max")
-            nc.vector.reduce_max(neg_max[:], s_ps[:], axis=mybir.AxisListType.X, negate=True)
-            e_sb = per_block.tile([BLOCK, BAND], F32, name="e_sb")
-            e_sum = per_block.tile([BLOCK, 1], F32, name="e_sum")
-            nc.scalar.activation(e_sb[:], s_ps[:], FUNC.Exp, bias=neg_max[:, 0:1], accum_out=e_sum[:, 0:1])
             inv_sum = per_block.tile([BLOCK, 1], F32, name="inv_sum")
-            nc.vector.reciprocal(inv_sum[:], e_sum[:])
+            nc.vector.reciprocal(inv_sum[:], e_sum[b][:])
             p_sb = per_block.tile([BLOCK, BAND], BF16, name="p_sb")
-            nc.vector.tensor_scalar(p_sb[:], e_sb[:], inv_sum[:, 0:1], None, op0=ALU.mult)
-
+            nc.vector.tensor_scalar(p_sb[:], e_sb[b][:], inv_sum[:, 0:1], None, op0=ALU.mult)
             pT_ps = other_banks.tile([BLOCK, BAND], BF16, name="pT_ps", tag="bank")
             for i in range(BAND_BLOCKS):
                 cols = slice(i * BLOCK, (i + 1) * BLOCK)
                 nc.tensor.transpose(pT_ps[:, cols], p_sb[:, cols], identity[:])
-            pT_sb = per_block.tile([BLOCK, BAND], BF16, name="pT_sb")
-            nc.scalar.copy(pT_sb[:], pT_ps[:])
+            nc.scalar.copy(pT_sb[b][:], pT_ps[:])
 
+        for b in range(N_BLOCKS):
             o_ps = other_banks.tile([D, BLOCK], F32, name="o_ps", tag="bank")
             for i in range(BAND_BLOCKS):
                 c = (b - HALF // BLOCK + i) % N_BLOCKS
                 nc.tensor.matmul(
                     o_ps[:],
                     vT_sb[:, c * BLOCK : (c + 1) * BLOCK],
-                    pT_sb[:, i * BLOCK : (i + 1) * BLOCK],
+                    pT_sb[b][:, i * BLOCK : (i + 1) * BLOCK],
                     start=(i == 0),
                     stop=(i == BAND_BLOCKS - 1),
                 )

@@ -13,6 +13,7 @@ BLOCK = 128
 N_BLOCKS = N // BLOCK
 BAND = BLOCK + 2 * HALF
 BAND_BLOCKS = BAND // BLOCK
+PSUM_BANKS = 8
 N_WARM = 14
 MASKED = -1.0e30
 
@@ -33,19 +34,21 @@ def tile_slidingwindowattention_kernel(tc, x, wq, bq, wk, wv, bv, offs, out):
     with (
         tc.tile_pool(name="held", bufs=1) as held,
         tc.tile_pool(name="per_block", bufs=N_BLOCKS) as per_block,
-        tc.psum_pool(name="score_banks", bufs=N_BLOCKS) as score_banks,
-        tc.psum_pool(name="other_banks", bufs=8 - N_BLOCKS) as other_banks,
+        tc.psum_pool(name="banks", bufs=PSUM_BANKS) as banks,
     ):
+        def bank(shape, dtype, name):
+            return banks.tile(shape, dtype, name=name, tag="bank")
+
         x_sb = held.tile([D, N], BF16, name="x_sb")
         nc.sync.dma_start(x_sb[:], x)
         offsets = held.tile([D, N // 16], U16, name="offsets")
         nc.sync.dma_start(offsets[:], offs)
+        wk_sb = held.tile([D, D], BF16, name="wk_sb")
+        nc.scalar.dma_start(wk_sb[:], wk)
         wq_sb = held.tile([D, D], BF16, name="wq_sb")
         nc.scalar.dma_start(wq_sb[:], wq)
         bq_sb = held.tile([D, 1], F32, name="bq_sb")
-        nc.scalar.dma_start(bq_sb[:], bq)
-        wk_sb = held.tile([D, D], BF16, name="wk_sb")
-        nc.sync.dma_start(wk_sb[:], wk)
+        nc.sync.dma_start(bq_sb[:], bq)
         wv_sb = held.tile([D, D], BF16, name="wv_sb")
         nc.scalar.dma_start(wv_sb[:], wv)
         bv_sb = held.tile([D, 1], F32, name="bv_sb")
@@ -53,7 +56,7 @@ def tile_slidingwindowattention_kernel(tc, x, wq, bq, wk, wv, bv, offs, out):
 
         zeros = held.tile([D, BLOCK], BF16, name="zeros")
         nc.vector.memset(zeros[:], 0.0)
-        warm_ps = other_banks.tile([D, BLOCK], F32, name="warm_ps", tag="bank")
+        warm_ps = bank([D, BLOCK], F32, "warm_ps")
         for w in range(N_WARM):
             nc.tensor.matmul(warm_ps[:], zeros[:], zeros[:], start=True, stop=True)
 
@@ -65,28 +68,33 @@ def tile_slidingwindowattention_kernel(tc, x, wq, bq, wk, wv, bv, offs, out):
         nc.gpsimd.iota(ahead[:], pattern=[[1, BLOCK]], base=0, channel_multiplier=-1)
         identity = held.tile([BLOCK, BLOCK], BF16, name="identity")
         nc.vector.tensor_scalar(identity[:], ahead[:], 0.0, None, op0=ALU.is_equal)
+        identity_f32 = held.tile([BLOCK, BLOCK], F32, name="identity_f32")
+        nc.vector.tensor_scalar(identity_f32[:], ahead[:], 0.0, None, op0=ALU.is_equal)
 
         band_mask = held.tile([BLOCK, BAND], BF16, name="band_mask")
         nc.vector.tensor_scalar(band_mask[:, 0:BLOCK], ahead[:], 0.0, MASKED, op0=ALU.is_lt, op1=ALU.mult)
         nc.vector.memset(band_mask[:, BLOCK : BAND - BLOCK], 0.0)
         nc.vector.tensor_scalar(band_mask[:, BAND - BLOCK : BAND], ahead[:], 0.0, MASKED, op0=ALU.is_gt, op1=ALU.mult)
 
-        q_ps = other_banks.tile([D, N], F32, name="q_ps", tag="bank")
-        nc.tensor.matmul(q_ps[:], wq_sb[:], x_sb[:].indirect(offsets[:]), start=True, stop=True)
-        k_ps = other_banks.tile([D, N], F32, name="k_ps", tag="bank")
+        k_ps = bank([D, N], F32, "k_ps")
         nc.tensor.matmul(k_ps[:], wk_sb[:], x_sb[:].indirect(offsets[:]), start=True, stop=True)
-        v_ps = other_banks.tile([D, N], F32, name="v_ps", tag="bank")
+        q_ps = bank([D, N], F32, "q_ps")
+        nc.tensor.matmul(q_ps[:], wq_sb[:], x_sb[:].indirect(offsets[:]), start=True, stop=True)
+        v_ps = bank([D, N], F32, "v_ps")
         nc.tensor.matmul(v_ps[:], wv_sb[:], x_sb[:].indirect(offsets[:]), start=True, stop=True)
 
-        q_sb = held.tile([D, N], BF16, name="q_sb")
-        nc.vector.tensor_scalar(q_sb[:], q_ps[:], bq_sb[:, 0:1], 1.0 / math.sqrt(D), op0=ALU.add, op1=ALU.mult)
         k_sb = held.tile([D, N], BF16, name="k_sb")
         nc.scalar.copy(k_sb[:], k_ps[:])
+        q_sb = held.tile([D, N], BF16, name="q_sb")
+        for cols in (slice(0, BLOCK), slice(BLOCK, N)):
+            nc.vector.tensor_scalar(
+                q_sb[:, cols], q_ps[:, cols], bq_sb[:, 0:1], 1.0 / math.sqrt(D), op0=ALU.add, op1=ALU.mult
+            )
         v_sb = held.tile([D, N], BF16, name="v_sb")
-        nc.vector.tensor_scalar(v_sb[:], v_ps[:], bv_sb[:, 0:1], None, op0=ALU.add)
+        nc.scalar.activation(v_sb[:], v_ps[:], FUNC.Identity, bias=bv_sb[:, 0:1])
 
 
-        s_ps = [score_banks.tile([BLOCK, BAND], F32, name="s_ps") for b in range(N_BLOCKS)]
+        s_ps = [bank([BLOCK, BAND], F32, "s_ps") for b in range(N_BLOCKS)]
         for b in range(N_BLOCKS):
             for at, first, width in unwrapped_runs(b * BLOCK - HALF, BAND, N):
                 nc.tensor.matmul(
@@ -98,12 +106,12 @@ def tile_slidingwindowattention_kernel(tc, x, wq, bq, wk, wv, bv, offs, out):
                 )
             nc.tensor.matmul(s_ps[b][:], identity[:], band_mask[:], start=False, stop=True)
 
-        vT_ps = other_banks.tile([BLOCK, N], BF16, name="vT_ps", tag="bank")
+        vT_ps = bank([BLOCK, N], BF16, "vT_ps")
         for c in range(N_BLOCKS):
             cols = slice(c * BLOCK, (c + 1) * BLOCK)
             nc.tensor.transpose(vT_ps[:, cols], v_sb[:, cols], identity[:])
 
-        e_sb = [per_block.tile([BLOCK, BAND], F32, name="e_sb") for b in range(N_BLOCKS)]
+        e_sb = [per_block.tile([BLOCK, BAND], BF16, name="e_sb") for b in range(N_BLOCKS)]
         e_sum = [per_block.tile([BLOCK, 1], F32, name="e_sum") for b in range(N_BLOCKS)]
         for b in range(N_BLOCKS):
             neg_max = per_block.tile([BLOCK, 1], F32, name="neg_max")
@@ -111,31 +119,33 @@ def tile_slidingwindowattention_kernel(tc, x, wq, bq, wk, wv, bv, offs, out):
             nc.scalar.activation(e_sb[b][:], s_ps[b][:], FUNC.Exp, bias=neg_max[:, 0:1], accum_out=e_sum[b][:, 0:1])
 
         vT_sb = held.tile([BLOCK, N], BF16, name="vT_sb")
-        nc.vector.tensor_copy(vT_sb[:], vT_ps[:])
+        nc.scalar.copy(vT_sb[:], vT_ps[:])
 
-        pT_sb = [per_block.tile([BLOCK, BAND], BF16, name="pT_sb") for b in range(N_BLOCKS)]
+        eT_sb = [per_block.tile([BLOCK, BAND], BF16, name="eT_sb") for b in range(N_BLOCKS)]
+        inv_rows = [per_block.tile([D, BLOCK], F32, name="inv_rows") for b in range(N_BLOCKS)]
         for b in range(N_BLOCKS):
-            inv_sum = per_block.tile([BLOCK, 1], F32, name="inv_sum")
-            nc.vector.reciprocal(inv_sum[:], e_sum[b][:])
-            p_sb = per_block.tile([BLOCK, BAND], BF16, name="p_sb")
-            nc.vector.tensor_scalar(p_sb[:], e_sb[b][:], inv_sum[:, 0:1], None, op0=ALU.mult)
-            pT_ps = other_banks.tile([BLOCK, BAND], BF16, name="pT_ps", tag="bank")
+            eT_ps = bank([BLOCK, BAND], BF16, "eT_ps")
             for i in range(BAND_BLOCKS):
                 cols = slice(i * BLOCK, (i + 1) * BLOCK)
-                nc.tensor.transpose(pT_ps[:, cols], p_sb[:, cols], identity[:])
-            nc.scalar.copy(pT_sb[b][:], pT_ps[:])
+                nc.tensor.transpose(eT_ps[:, cols], e_sb[b][:, cols], identity[:])
+            inv_sum = per_block.tile([BLOCK, 1], F32, name="inv_sum")
+            nc.vector.reciprocal(inv_sum[:], e_sum[b][:])
+            inv_ps = bank([D, BLOCK], F32, "inv_ps")
+            nc.tensor.transpose(inv_ps[:], inv_sum[:, 0:1].to_broadcast([BLOCK, D]), identity_f32[:])
+            nc.vector.tensor_copy(eT_sb[b][:], eT_ps[:])
+            nc.scalar.copy(inv_rows[b][:], inv_ps[:])
 
         for b in range(N_BLOCKS):
-            o_ps = other_banks.tile([D, BLOCK], F32, name="o_ps", tag="bank")
+            o_ps = bank([D, BLOCK], F32, "o_ps")
             for i in range(BAND_BLOCKS):
                 c = (b - HALF // BLOCK + i) % N_BLOCKS
                 nc.tensor.matmul(
                     o_ps[:],
                     vT_sb[:, c * BLOCK : (c + 1) * BLOCK],
-                    pT_sb[b][:, i * BLOCK : (i + 1) * BLOCK],
+                    eT_sb[b][:, i * BLOCK : (i + 1) * BLOCK],
                     start=(i == 0),
                     stop=(i == BAND_BLOCKS - 1),
                 )
             o_sb = per_block.tile([D, BLOCK], F32, name="o_sb")
-            nc.vector.tensor_copy(o_sb[:], o_ps[:])
+            nc.vector.tensor_tensor(o_sb[:], o_ps[:], inv_rows[b][:], op=ALU.mult)
             nc.sync.dma_start(out[:, b * BLOCK : (b + 1) * BLOCK], o_sb[:])

@@ -54,11 +54,11 @@ def tile_slidingwindowattention_kernel(tc, x, wq, bq, wk, wv, bv, offs, out):
         bv_sb = held.tile([D, 1], F32, name="bv_sb")
         nc.sync.dma_start(bv_sb[:], bv)
 
-        zeros = held.tile([D, BLOCK], BF16, name="zeros")
-        nc.vector.memset(zeros[:], 0.0)
+        ones = held.tile([D, BLOCK], BF16, name="ones")
+        nc.vector.memset(ones[:], 1.0)
         warm_ps = bank([D, BLOCK], F32, "warm_ps")
         for w in range(N_WARM):
-            nc.tensor.matmul(warm_ps[:], zeros[:], zeros[:], start=True, stop=True)
+            nc.tensor.matmul(warm_ps[:], ones[:], ones[:], start=True, stop=True)
 
         scratch = held.tile([D, 1], F32, name="scratch")
         nc.vector.memset(scratch[:], 0.0)
@@ -109,7 +109,7 @@ def tile_slidingwindowattention_kernel(tc, x, wq, bq, wk, wv, bv, offs, out):
         vT_ps = bank([BLOCK, N], BF16, "vT_ps")
         for c in range(N_BLOCKS):
             cols = slice(c * BLOCK, (c + 1) * BLOCK)
-            nc.tensor.transpose(vT_ps[:, cols], v_sb[:, cols], identity[:])
+            nc.tensor.matmul(vT_ps[:, cols], v_sb[:, cols], identity[:], start=True, stop=True)
 
         e_sb = [per_block.tile([BLOCK, BAND], BF16, name="e_sb") for b in range(N_BLOCKS)]
         e_sum = [per_block.tile([BLOCK, 1], F32, name="e_sum") for b in range(N_BLOCKS)]
@@ -127,7 +127,7 @@ def tile_slidingwindowattention_kernel(tc, x, wq, bq, wk, wv, bv, offs, out):
             eT_ps = bank([BLOCK, BAND], BF16, "eT_ps")
             for i in range(BAND_BLOCKS):
                 cols = slice(i * BLOCK, (i + 1) * BLOCK)
-                nc.tensor.transpose(eT_ps[:, cols], e_sb[b][:, cols], identity[:])
+                nc.tensor.matmul(eT_ps[:, cols], e_sb[b][:, cols], identity[:], start=True, stop=True)
             inv_sum = per_block.tile([BLOCK, 1], F32, name="inv_sum")
             nc.vector.reciprocal(inv_sum[:], e_sum[b][:])
             inv_ps = bank([D, BLOCK], F32, "inv_ps")

@@ -119,7 +119,7 @@ def tile_slidingwindowattention_kernel(tc, x, wq, bq, wk, wv, bv, offs, out):
             nc.scalar.activation(e_sb[b][:], s_ps[b][:], FUNC.Exp, bias=neg_max[:, 0:1], accum_out=e_sum[b][:, 0:1])
 
         vT_sb = held.tile([BLOCK, N], BF16, name="vT_sb")
-        nc.scalar.copy(vT_sb[:], vT_ps[:])
+        nc.vector.tensor_copy(vT_sb[:], vT_ps[:])
 
         eT_sb = [per_block.tile([BLOCK, BAND], BF16, name="eT_sb") for b in range(N_BLOCKS)]
         inv_rows = [per_block.tile([D, BLOCK], F32, name="inv_rows") for b in range(N_BLOCKS)]

@@ -96,15 +96,15 @@ def tile_slidingwindowattention_kernel(tc, x, wq, bq, wk, wv, bv, offs, out):
 
         s_ps = [bank([BLOCK, BAND], F32, "s_ps") for b in range(N_BLOCKS)]
         for b in range(N_BLOCKS):
+            nc.tensor.matmul(s_ps[b][:], identity[:], band_mask[:], start=True, stop=False)
             for at, first, width in unwrapped_runs(b * BLOCK - HALF, BAND, N):
                 nc.tensor.matmul(
                     s_ps[b][:, at : at + width],
                     q_sb[:, b * BLOCK : (b + 1) * BLOCK],
                     k_sb[:, first : first + width],
-                    start=(at == 0),
-                    stop=False,
+                    start=False,
+                    stop=(at + width == BAND),
                 )
-            nc.tensor.matmul(s_ps[b][:], identity[:], band_mask[:], start=False, stop=True)
 
         vT_ps = bank([BLOCK, N], BF16, "vT_ps")
         for c in range(N_BLOCKS):

@@ -34,6 +34,7 @@ def tile_slidingwindowattention_kernel(tc, x, wq, bq, wk, wv, bv, offs, out):
     with (
         tc.tile_pool(name="held", bufs=1) as held,
         tc.tile_pool(name="per_block", bufs=N_BLOCKS) as per_block,
+        tc.tile_pool(name="per_copy", bufs=N_BLOCKS - 1 + BAND_BLOCKS) as per_copy,
         tc.psum_pool(name="banks", bufs=PSUM_BANKS) as banks,
     ):
         def bank(shape, dtype, name):
@@ -121,18 +122,30 @@ def tile_slidingwindowattention_kernel(tc, x, wq, bq, wk, wv, bv, offs, out):
         vT_sb = held.tile([BLOCK, N], BF16, name="vT_sb")
         nc.vector.tensor_copy(vT_sb[:], vT_ps[:])
 
-        eT_sb = [per_block.tile([BLOCK, BAND], BF16, name="eT_sb") for b in range(N_BLOCKS)]
+        eT_sb = [[] for b in range(N_BLOCKS)]
         inv_rows = [per_block.tile([D, BLOCK], F32, name="inv_rows") for b in range(N_BLOCKS)]
         for b in range(N_BLOCKS):
-            eT_ps = bank([BLOCK, BAND], BF16, "eT_ps")
+            flips_to_a_bank = BAND_BLOCKS if b < N_BLOCKS - 1 else 1
+            eT_ps = []
             for i in range(BAND_BLOCKS):
-                cols = slice(i * BLOCK, (i + 1) * BLOCK)
-                nc.tensor.matmul(eT_ps[:, cols], e_sb[b][:, cols], identity[:], start=True, stop=True)
+                if i % flips_to_a_bank == 0:
+                    eT_ps.append(bank([BLOCK, flips_to_a_bank * BLOCK], BF16, "eT_ps"))
+                at = (i % flips_to_a_bank) * BLOCK
+                nc.tensor.matmul(
+                    eT_ps[-1][:, at : at + BLOCK],
+                    e_sb[b][:, i * BLOCK : (i + 1) * BLOCK],
+                    identity[:],
+                    start=True,
+                    stop=True,
+                )
             inv_sum = per_block.tile([BLOCK, 1], F32, name="inv_sum")
             nc.vector.reciprocal(inv_sum[:], e_sum[b][:])
             inv_ps = bank([D, BLOCK], F32, "inv_ps")
             nc.tensor.transpose(inv_ps[:], inv_sum[:, 0:1].to_broadcast([BLOCK, D]), identity_f32[:])
-            nc.vector.tensor_copy(eT_sb[b][:], eT_ps[:])
+            for flipped in eT_ps:
+                copied = per_copy.tile([BLOCK, flips_to_a_bank * BLOCK], BF16, name="copied")
+                nc.vector.tensor_copy(copied[:], flipped[:])
+                eT_sb[b].extend(copied[:, at : at + BLOCK] for at in range(0, flips_to_a_bank * BLOCK, BLOCK))
             nc.scalar.copy(inv_rows[b][:], inv_ps[:])
 
         for b in range(N_BLOCKS):
@@ -142,7 +155,7 @@ def tile_slidingwindowattention_kernel(tc, x, wq, bq, wk, wv, bv, offs, out):
                 nc.tensor.matmul(
                     o_ps[:],
                     vT_sb[:, c * BLOCK : (c + 1) * BLOCK],
-                    eT_sb[b][:, i * BLOCK : (i + 1) * BLOCK],
+                    eT_sb[b][i],
                     start=(i == 0),
                     stop=(i == BAND_BLOCKS - 1),
                 )

@@ -119,6 +119,10 @@ def tile_slidingwindowattention_kernel(tc, x, wq, bq, wk, wv, bv, offs, out):
             nc.vector.reduce_max(neg_max[:], s_ps[b][:], axis=mybir.AxisListType.X, negate=True)
             nc.scalar.activation(e_sb[b][:], s_ps[b][:], FUNC.Exp, bias=neg_max[:, 0:1], accum_out=e_sum[b][:, 0:1])
 
+        inv_sum = [per_block.tile([BLOCK, 1], F32, name="inv_sum") for b in range(N_BLOCKS)]
+        for b in range(N_BLOCKS):
+            nc.vector.reciprocal(inv_sum[b][:], e_sum[b][:])
+
         vT_sb = held.tile([BLOCK, N], BF16, name="vT_sb")
         nc.vector.tensor_copy(vT_sb[:], vT_ps[:])
 
@@ -138,10 +142,8 @@ def tile_slidingwindowattention_kernel(tc, x, wq, bq, wk, wv, bv, offs, out):
                     start=True,
                     stop=True,
                 )
-            inv_sum = per_block.tile([BLOCK, 1], F32, name="inv_sum")
-            nc.vector.reciprocal(inv_sum[:], e_sum[b][:])
             inv_ps = bank([D, BLOCK], F32, "inv_ps")
-            nc.tensor.transpose(inv_ps[:], inv_sum[:, 0:1].to_broadcast([BLOCK, D]), identity_f32[:])
+            nc.tensor.transpose(inv_ps[:], inv_sum[b][:, 0:1].to_broadcast([BLOCK, D]), identity_f32[:])
             for flipped in eT_ps:
                 copied = per_copy.tile([BLOCK, flips_to_a_bank * BLOCK], BF16, name="copied")
                 nc.vector.tensor_copy(copied[:], flipped[:])

@@ -14,7 +14,7 @@ N_BLOCKS = N // BLOCK
 BAND = BLOCK + 2 * HALF
 BAND_BLOCKS = BAND // BLOCK
 PSUM_BANKS = 8
-N_WARM = 14
+N_WARM = 7
 MASKED = -1.0e30
 
 FLOPS = 3 * 2 * D * D * N + 2 * 2 * D * N * (2 * HALF + 1)

@@ -2,7 +2,7 @@ import math
 
 import concourse.mybir as mybir
 
-BF16, F32, I32, U16 = mybir.dt.bfloat16, mybir.dt.float32, mybir.dt.int32, mybir.dt.uint16
+BF16, F32, U16 = mybir.dt.bfloat16, mybir.dt.float32, mybir.dt.uint16
 FUNC = mybir.ActivationFunctionType
 ALU = mybir.AluOpType
 
@@ -65,17 +65,26 @@ def tile_slidingwindowattention_kernel(tc, x, wq, bq, wk, wv, bv, offs, out):
         nc.vector.memset(scratch[:], 0.0)
         nc.scalar.activation(scratch[:], scratch[:], FUNC.Exp)
 
-        ahead = held.tile([BLOCK, BLOCK], I32, name="ahead")
-        nc.gpsimd.iota(ahead[:], pattern=[[1, BLOCK]], base=0, channel_multiplier=-1)
         identity = held.tile([BLOCK, BLOCK], BF16, name="identity")
-        nc.vector.tensor_scalar(identity[:], ahead[:], 0.0, None, op0=ALU.is_equal)
-        identity_f32 = held.tile([BLOCK, BLOCK], F32, name="identity_f32")
-        nc.vector.tensor_scalar(identity_f32[:], ahead[:], 0.0, None, op0=ALU.is_equal)
+        nc.gpsimd.affine_select(
+            out=identity[:], in_=ones[:], pattern=[[1, BLOCK]], compare_op=ALU.is_equal, fill=0.0, base=0, channel_multiplier=-1
+        )
 
         band_mask = held.tile([BLOCK, BAND], BF16, name="band_mask")
-        nc.vector.tensor_scalar(band_mask[:, 0:BLOCK], ahead[:], 0.0, MASKED, op0=ALU.is_lt, op1=ALU.mult)
-        nc.vector.memset(band_mask[:, BLOCK : BAND - BLOCK], 0.0)
-        nc.vector.tensor_scalar(band_mask[:, BAND - BLOCK : BAND], ahead[:], 0.0, MASKED, op0=ALU.is_gt, op1=ALU.mult)
+        nc.vector.memset(band_mask[:], 0.0)
+        for cols, sign in ((slice(0, BLOCK), 1), (slice(BAND - BLOCK, BAND), -1)):
+            nc.gpsimd.affine_select(
+                out=band_mask[:, cols],
+                in_=band_mask[:, cols],
+                pattern=[[sign, BLOCK]],
+                compare_op=ALU.is_ge,
+                fill=MASKED,
+                base=0,
+                channel_multiplier=-sign,
+            )
+
+        identity_f32 = held.tile([BLOCK, BLOCK], F32, name="identity_f32")
+        nc.vector.tensor_copy(identity_f32[:], identity[:])
 
         k_ps = bank([D, N], F32, "k_ps")
         nc.tensor.matmul(k_ps[:], wk_sb[:], x_sb[:].indirect(offsets[:]), start=True, stop=True)

@@ -136,8 +136,8 @@ def tile_slidingwindowattention_kernel(tc, x, wq, bq, wk, wv, bv, offs, out):
         nc.vector.tensor_copy(vT_sb[:], vT_ps[:])
 
         eT_sb = [[] for b in range(N_BLOCKS)]
-        inv_rows = [per_block.tile([D, BLOCK], F32, name="inv_rows") for b in range(N_BLOCKS)]
-        for b in range(N_BLOCKS):
+
+        def flip(b):
             flips_to_a_bank = BAND_BLOCKS if b < N_BLOCKS - 1 else 1
             eT_ps = []
             for i in range(BAND_BLOCKS):
@@ -151,25 +151,50 @@ def tile_slidingwindowattention_kernel(tc, x, wq, bq, wk, wv, bv, offs, out):
                     start=True,
                     stop=True,
                 )
-            inv_ps = bank([D, BLOCK], F32, "inv_ps")
-            nc.tensor.transpose(inv_ps[:], inv_sum[b][:, 0:1].to_broadcast([BLOCK, D]), identity_f32[:])
             for flipped in eT_ps:
                 copied = per_copy.tile([BLOCK, flips_to_a_bank * BLOCK], BF16, name="copied")
                 nc.vector.tensor_copy(copied[:], flipped[:])
                 eT_sb[b].extend(copied[:, at : at + BLOCK] for at in range(0, flips_to_a_bank * BLOCK, BLOCK))
-            nc.scalar.copy(inv_rows[b][:], inv_ps[:])
 
-        for b in range(N_BLOCKS):
-            o_ps = bank([D, BLOCK], F32, "o_ps")
+        inv_rows = [per_block.tile([D, BLOCK], F32, name="inv_rows") for b in range(N_BLOCKS)]
+
+        inv_ps = [None] * N_BLOCKS
+
+        def spread_inverse(b):
+            inv_ps[b] = bank([D, BLOCK], F32, "inv_ps")
+            nc.tensor.transpose(inv_ps[b][:], inv_sum[b][:, 0:1].to_broadcast([BLOCK, D]), identity_f32[:])
+
+        o_ps = [None] * N_BLOCKS
+
+        def weigh(b):
+            o_ps[b] = bank([D, BLOCK], F32, "o_ps")
             for i in range(BAND_BLOCKS):
                 c = (b - HALF // BLOCK + i) % N_BLOCKS
                 nc.tensor.matmul(
-                    o_ps[:],
+                    o_ps[b][:],
                     vT_sb[:, c * BLOCK : (c + 1) * BLOCK],
                     eT_sb[b][i],
                     start=(i == 0),
                     stop=(i == BAND_BLOCKS - 1),
                 )
+
+        def finish(b):
+            nc.scalar.copy(inv_rows[b][:], inv_ps[b][:])
             o_sb = per_block.tile([D, BLOCK], F32, name="o_sb")
-            nc.vector.tensor_tensor(o_sb[:], o_ps[:], inv_rows[b][:], op=ALU.mult)
+            nc.vector.tensor_tensor(o_sb[:], o_ps[b][:], inv_rows[b][:], op=ALU.mult)
             nc.sync.dma_start(out[:, b * BLOCK : (b + 1) * BLOCK], o_sb[:])
+
+        flip(0)
+        flip(1)
+        spread_inverse(0)
+        flip(2)
+        spread_inverse(1)
+        weigh(0)
+        flip(3)
+        spread_inverse(2)
+        weigh(1)
+        spread_inverse(3)
+        weigh(2)
+        weigh(3)
+        for b in range(N_BLOCKS):
+            finish(b)

@@ -14,6 +14,7 @@ N_BLOCKS = N // BLOCK
 BAND = BLOCK + 2 * HALF
 BAND_BLOCKS = BAND // BLOCK
 PSUM_BANKS = 8
+SQUARE = 32
 N_WARM = 7
 MASKED = -1.0e30
 
@@ -65,23 +66,27 @@ def tile_slidingwindowattention_kernel(tc, x, wq, bq, wk, wv, bv, offs, out):
         nc.vector.memset(scratch[:], 0.0)
         nc.scalar.activation(scratch[:], scratch[:], FUNC.Exp)
 
-        identity = held.tile([BLOCK, BLOCK], BF16, name="identity")
-        nc.gpsimd.affine_select(
-            out=identity[:], in_=ones[:], pattern=[[1, BLOCK]], compare_op=ALU.is_equal, fill=0.0, base=0, channel_multiplier=-1
+        ones_f32 = held.tile([BLOCK, BLOCK], F32, name="ones_f32")
+        nc.vector.memset(ones_f32[:], 1.0)
+        before = held.tile([BLOCK, 1], F32, name="before")
+        for first in range(0, BLOCK, SQUARE):
+            nc.vector.memset(before[first : first + SQUARE, :], first - 1.0)
+        count = held.tile([BLOCK, SQUARE], F32, name="count", align_bytes=64)
+        nc.vector.tensor_tensor_scan(
+            count[:], ones_f32[:, 0:SQUARE], ones_f32[:, 0:SQUARE], before[:, 0:1], op0=ALU.mult, op1=ALU.add
         )
+        own = held.tile([BLOCK, SQUARE], F32, name="own", align_bytes=64)
+        nc.vector.transpose(own[:], count[:])
+        column = held.tile([BLOCK, BLOCK], F32, name="column")
+        nc.vector.tensor_tensor_scan(column[:], ones_f32[:], ones_f32[:], -1.0, op0=ALU.mult, op1=ALU.add)
+
+        identity = held.tile([BLOCK, BLOCK], BF16, name="identity")
+        nc.vector.tensor_scalar(identity[:], column[:], own[:, 0:1], None, op0=ALU.is_equal)
 
         band_mask = held.tile([BLOCK, BAND], BF16, name="band_mask")
-        nc.vector.memset(band_mask[:], 0.0)
-        for cols, sign in ((slice(0, BLOCK), 1), (slice(BAND - BLOCK, BAND), -1)):
-            nc.gpsimd.affine_select(
-                out=band_mask[:, cols],
-                in_=band_mask[:, cols],
-                pattern=[[sign, BLOCK]],
-                compare_op=ALU.is_ge,
-                fill=MASKED,
-                base=0,
-                channel_multiplier=-sign,
-            )
+        nc.vector.memset(band_mask[:, BLOCK : BAND - BLOCK], 0.0)
+        for cols, beyond in ((slice(0, BLOCK), ALU.is_lt), (slice(BAND - BLOCK, BAND), ALU.is_gt)):
+            nc.vector.tensor_scalar(band_mask[:, cols], column[:], own[:, 0:1], MASKED, op0=beyond, op1=ALU.mult)
 
         identity_f32 = held.tile([BLOCK, BLOCK], F32, name="identity_f32")
         nc.vector.tensor_copy(identity_f32[:], identity[:])
@@ -106,15 +111,19 @@ def tile_slidingwindowattention_kernel(tc, x, wq, bq, wk, wv, bv, offs, out):
 
         s_ps = [bank([BLOCK, BAND], F32, "s_ps") for b in range(N_BLOCKS)]
         for b in range(N_BLOCKS):
-            nc.tensor.matmul(s_ps[b][:], identity[:], band_mask[:], start=True, stop=False)
+            mask_first = b == 0
+            if mask_first:
+                nc.tensor.matmul(s_ps[b][:], identity[:], band_mask[:], start=True, stop=False)
             for at, first, width in unwrapped_runs(b * BLOCK - HALF, BAND, N):
                 nc.tensor.matmul(
                     s_ps[b][:, at : at + width],
                     q_sb[:, b * BLOCK : (b + 1) * BLOCK],
                     k_sb[:, first : first + width],
-                    start=False,
-                    stop=(at + width == BAND),
+                    start=(at == 0 and not mask_first),
+                    stop=(at + width == BAND and mask_first),
                 )
+            if not mask_first:
+                nc.tensor.matmul(s_ps[b][:], identity[:], band_mask[:], start=False, stop=True)
 
         vT_ps = bank([BLOCK, N], BF16, "vT_ps")
         for c in range(N_BLOCKS):

@@ -109,6 +109,9 @@ def tile_slidingwindowattention_kernel(tc, x, wq, bq, wk, wv, bv, offs, out):
         nc.scalar.activation(v_sb[:], v_ps[:], FUNC.Identity, bias=bv_sb[:, 0:1])
 
 
+        def outer_blocks(band):
+            return band[:].rearrange("p (i c) -> p i c", c=BLOCK)[:, 0:BAND_BLOCKS:2, :]
+
         s_ps = [bank([BLOCK, BAND], F32, "s_ps") for b in range(N_BLOCKS)]
         for b in range(N_BLOCKS):
             mask_first = b == 0
@@ -123,7 +126,7 @@ def tile_slidingwindowattention_kernel(tc, x, wq, bq, wk, wv, bv, offs, out):
                     stop=(at + width == BAND and mask_first),
                 )
             if not mask_first:
-                nc.tensor.matmul(s_ps[b][:], identity[:], band_mask[:], start=False, stop=True)
+                nc.tensor.matmul(outer_blocks(s_ps[b]), identity[:], outer_blocks(band_mask), start=False, stop=True)
 
         vT_ps = bank([BLOCK, N], BF16, "vT_ps")
         for c in range(N_BLOCKS):

@@ -15,7 +15,7 @@ BAND = BLOCK + 2 * HALF
 BAND_BLOCKS = BAND // BLOCK
 PSUM_BANKS = 8
 SQUARE = 32
-N_WARM = 7
+N_WARM = 14
 MASKED = -1.0e30
 
 FLOPS = 3 * 2 * D * D * N + 2 * 2 * D * N * (2 * HALF + 1)

import math

import concourse.mybir as mybir

BF16, F32, U16 = mybir.dt.bfloat16, mybir.dt.float32, mybir.dt.uint16
FUNC = mybir.ActivationFunctionType
ALU = mybir.AluOpType

D = 128
N = 512
HALF = 128
BLOCK = 128
N_BLOCKS = N // BLOCK
BAND = BLOCK + 2 * HALF
BAND_BLOCKS = BAND // BLOCK
PSUM_BANKS = 8
SQUARE = 32
N_WARM = 14
MASKED = -1.0e30

FLOPS = 3 * 2 * D * D * N + 2 * 2 * D * N * (2 * HALF + 1)


def unwrapped_runs(first, width, ring):
    first = first % ring
    head = min(width, ring - first)
    runs = [(0, first, head)]
    if head < width:
        runs.append((head, 0, width - head))
    return runs


def tile_slidingwindowattention_kernel(tc, x, wq, bq, wk, wv, bv, offs, out):
    nc = tc.nc
    with (
        tc.tile_pool(name="held", bufs=1) as held,
        tc.tile_pool(name="per_block", bufs=N_BLOCKS) as per_block,
        tc.tile_pool(name="per_copy", bufs=N_BLOCKS - 1 + BAND_BLOCKS) as per_copy,
        tc.psum_pool(name="banks", bufs=PSUM_BANKS) as banks,
    ):
        def bank(shape, dtype, name):
            return banks.tile(shape, dtype, name=name, tag="bank")

        x_sb = held.tile([D, N], BF16, name="x_sb")
        nc.sync.dma_start(x_sb[:], x)
        offsets = held.tile([D, N // 16], U16, name="offsets")
        nc.sync.dma_start(offsets[:], offs)
        wk_sb = held.tile([D, D], BF16, name="wk_sb")
        nc.scalar.dma_start(wk_sb[:], wk)
        wq_sb = held.tile([D, D], BF16, name="wq_sb")
        nc.scalar.dma_start(wq_sb[:], wq)
        bq_sb = held.tile([D, 1], F32, name="bq_sb")
        nc.sync.dma_start(bq_sb[:], bq)
        wv_sb = held.tile([D, D], BF16, name="wv_sb")
        nc.scalar.dma_start(wv_sb[:], wv)
        bv_sb = held.tile([D, 1], F32, name="bv_sb")
        nc.sync.dma_start(bv_sb[:], bv)

        ones = held.tile([D, BLOCK], BF16, name="ones")
        nc.vector.memset(ones[:], 1.0)
        warm_ps = bank([D, BLOCK], F32, "warm_ps")
        for w in range(N_WARM):
            nc.tensor.matmul(warm_ps[:], ones[:], ones[:], start=True, stop=True)

        scratch = held.tile([D, 1], F32, name="scratch")
        nc.vector.memset(scratch[:], 0.0)
        nc.scalar.activation(scratch[:], scratch[:], FUNC.Exp)

        ones_f32 = held.tile([BLOCK, BLOCK], F32, name="ones_f32")
        nc.vector.memset(ones_f32[:], 1.0)
        before = held.tile([BLOCK, 1], F32, name="before")
        for first in range(0, BLOCK, SQUARE):
            nc.vector.memset(before[first : first + SQUARE, :], first - 1.0)
        count = held.tile([BLOCK, SQUARE], F32, name="count", align_bytes=64)
        nc.vector.tensor_tensor_scan(
            count[:], ones_f32[:, 0:SQUARE], ones_f32[:, 0:SQUARE], before[:, 0:1], op0=ALU.mult, op1=ALU.add
        )
        own = held.tile([BLOCK, SQUARE], F32, name="own", align_bytes=64)
        nc.vector.transpose(own[:], count[:])
        column = held.tile([BLOCK, BLOCK], F32, name="column")
        nc.vector.tensor_tensor_scan(column[:], ones_f32[:], ones_f32[:], -1.0, op0=ALU.mult, op1=ALU.add)

        identity = held.tile([BLOCK, BLOCK], BF16, name="identity")
        nc.vector.tensor_scalar(identity[:], column[:], own[:, 0:1], None, op0=ALU.is_equal)

        band_mask = held.tile([BLOCK, BAND], BF16, name="band_mask")
        nc.vector.memset(band_mask[:, BLOCK : BAND - BLOCK], 0.0)
        for cols, beyond in ((slice(0, BLOCK), ALU.is_lt), (slice(BAND - BLOCK, BAND), ALU.is_gt)):
            nc.vector.tensor_scalar(band_mask[:, cols], column[:], own[:, 0:1], MASKED, op0=beyond, op1=ALU.mult)

        identity_f32 = held.tile([BLOCK, BLOCK], F32, name="identity_f32")
        nc.vector.tensor_copy(identity_f32[:], identity[:])

        k_ps = bank([D, N], F32, "k_ps")
        nc.tensor.matmul(k_ps[:], wk_sb[:], x_sb[:].indirect(offsets[:]), start=True, stop=True)
        q_ps = bank([D, N], F32, "q_ps")
        nc.tensor.matmul(q_ps[:], wq_sb[:], x_sb[:].indirect(offsets[:]), start=True, stop=True)
        v_ps = bank([D, N], F32, "v_ps")
        nc.tensor.matmul(v_ps[:], wv_sb[:], x_sb[:].indirect(offsets[:]), start=True, stop=True)

        k_sb = held.tile([D, N], BF16, name="k_sb")
        nc.scalar.copy(k_sb[:], k_ps[:])
        q_sb = held.tile([D, N], BF16, name="q_sb")
        for cols in (slice(0, BLOCK), slice(BLOCK, N)):
            nc.vector.tensor_scalar(
                q_sb[:, cols], q_ps[:, cols], bq_sb[:, 0:1], 1.0 / math.sqrt(D), op0=ALU.add, op1=ALU.mult
            )
        v_sb = held.tile([D, N], BF16, name="v_sb")
        nc.scalar.activation(v_sb[:], v_ps[:], FUNC.Identity, bias=bv_sb[:, 0:1])


        def outer_blocks(band):
            return band[:].rearrange("p (i c) -> p i c", c=BLOCK)[:, 0:BAND_BLOCKS:2, :]

        s_ps = [bank([BLOCK, BAND], F32, "s_ps") for b in range(N_BLOCKS)]
        for b in range(N_BLOCKS):
            mask_first = b == 0
            if mask_first:
                nc.tensor.matmul(s_ps[b][:], identity[:], band_mask[:], start=True, stop=False)
            for at, first, width in unwrapped_runs(b * BLOCK - HALF, BAND, N):
                nc.tensor.matmul(
                    s_ps[b][:, at : at + width],
                    q_sb[:, b * BLOCK : (b + 1) * BLOCK],
                    k_sb[:, first : first + width],
                    start=(at == 0 and not mask_first),
                    stop=(at + width == BAND and mask_first),
                )
            if not mask_first:
                nc.tensor.matmul(outer_blocks(s_ps[b]), identity[:], outer_blocks(band_mask), start=False, stop=True)

        vT_ps = bank([BLOCK, N], BF16, "vT_ps")
        for c in range(N_BLOCKS):
            cols = slice(c * BLOCK, (c + 1) * BLOCK)
            nc.tensor.matmul(vT_ps[:, cols], v_sb[:, cols], identity[:], start=True, stop=True)

        e_sb = [per_block.tile([BLOCK, BAND], BF16, name="e_sb") for b in range(N_BLOCKS)]
        e_sum = [per_block.tile([BLOCK, 1], F32, name="e_sum") for b in range(N_BLOCKS)]
        for b in range(N_BLOCKS):
            neg_max = per_block.tile([BLOCK, 1], F32, name="neg_max")
            nc.vector.reduce_max(neg_max[:], s_ps[b][:], axis=mybir.AxisListType.X, negate=True)
            nc.scalar.activation(e_sb[b][:], s_ps[b][:], FUNC.Exp, bias=neg_max[:, 0:1], accum_out=e_sum[b][:, 0:1])

        inv_sum = [per_block.tile([BLOCK, 1], F32, name="inv_sum") for b in range(N_BLOCKS)]
        for b in range(N_BLOCKS):
            nc.vector.reciprocal(inv_sum[b][:], e_sum[b][:])

        vT_sb = held.tile([BLOCK, N], BF16, name="vT_sb")
        nc.vector.tensor_copy(vT_sb[:], vT_ps[:])

        eT_sb = [[] for b in range(N_BLOCKS)]

        def flip(b):
            flips_to_a_bank = BAND_BLOCKS if b < N_BLOCKS - 1 else 1
            eT_ps = []
            for i in range(BAND_BLOCKS):
                if i % flips_to_a_bank == 0:
                    eT_ps.append(bank([BLOCK, flips_to_a_bank * BLOCK], BF16, "eT_ps"))
                at = (i % flips_to_a_bank) * BLOCK
                nc.tensor.matmul(
                    eT_ps[-1][:, at : at + BLOCK],
                    e_sb[b][:, i * BLOCK : (i + 1) * BLOCK],
                    identity[:],
                    start=True,
                    stop=True,
                )
            for flipped in eT_ps:
                copied = per_copy.tile([BLOCK, flips_to_a_bank * BLOCK], BF16, name="copied")
                nc.vector.tensor_copy(copied[:], flipped[:])
                eT_sb[b].extend(copied[:, at : at + BLOCK] for at in range(0, flips_to_a_bank * BLOCK, BLOCK))

        inv_rows = [per_block.tile([D, BLOCK], F32, name="inv_rows") for b in range(N_BLOCKS)]

        inv_ps = [None] * N_BLOCKS

        def spread_inverse(b):
            inv_ps[b] = bank([D, BLOCK], F32, "inv_ps")
            nc.tensor.transpose(inv_ps[b][:], inv_sum[b][:, 0:1].to_broadcast([BLOCK, D]), identity_f32[:])

        o_ps = [None] * N_BLOCKS

        def weigh(b):
            o_ps[b] = bank([D, BLOCK], F32, "o_ps")
            for i in range(BAND_BLOCKS):
                c = (b - HALF // BLOCK + i) % N_BLOCKS
                nc.tensor.matmul(
                    o_ps[b][:],
                    vT_sb[:, c * BLOCK : (c + 1) * BLOCK],
                    eT_sb[b][i],
                    start=(i == 0),
                    stop=(i == BAND_BLOCKS - 1),
                )

        def finish(b):
            nc.scalar.copy(inv_rows[b][:], inv_ps[b][:])
            o_sb = per_block.tile([D, BLOCK], F32, name="o_sb")
            nc.vector.tensor_tensor(o_sb[:], o_ps[b][:], inv_rows[b][:], op=ALU.mult)
            nc.sync.dma_start(out[:, b * BLOCK : (b + 1) * BLOCK], o_sb[:])

        flip(0)
        flip(1)
        spread_inverse(0)
        flip(2)
        spread_inverse(1)
        weigh(0)
        flip(3)
        spread_inverse(2)
        weigh(1)
        spread_inverse(3)
        weigh(2)
        weigh(3)
        for b in range(N_BLOCKS):
            finish(b)
